import numpy as np
import ml_dtypes


def mxq(x, axis, fmt="e4m3"):
    dtype, down = {"e4m3": (ml_dtypes.float8_e4m3fn, 7), "e5m2": (ml_dtypes.float8_e5m2, 14)}[fmt]
    v = np.moveaxis(np.asarray(x, np.float32).astype(ml_dtypes.bfloat16).astype(np.float64), axis, -1)
    blocks = v.reshape(v.shape[:-1] + (-1, 32))
    amax = np.abs(blocks).max(-1, keepdims=True)
    byte = np.maximum(np.where(amax > 0, np.frexp(amax)[1] - 1 + 127, 0) - down, 1)
    scale = np.exp2(byte - 127.0)
    codes = (blocks / scale).astype(np.float32).astype(dtype).astype(np.float64)
    return np.moveaxis((codes * scale).reshape(v.shape), -1, axis)


WIDE = False


def mx_kscale(k):
    if not WIDE:
        return np.ones(k)
    levels = np.array([10, -10, 5, -5, 0])
    a = np.random.permutation(np.resize(levels, k // 512 * 4)).reshape(k // 512, 4)
    idx = np.arange(k)
    return np.exp2(a[idx // 512, idx % 128 // 32])


BF16 = ml_dtypes.bfloat16


def bf(x):
    return np.asarray(x, np.float32).astype(BF16)


def f64(x):
    return np.asarray(x).astype(np.float64)


E2M1 = np.array([0.0, 0.5, 1.0, 1.5, 2.0, 3.0, 4.0, 6.0, -0.0, -0.5, -1.0, -1.5, -2.0, -3.0, -4.0, -6.0])


def pack_weight(w, fmt):
    k, n = w.shape
    w = f64(bf(w)).reshape(k // 32, 32, n)
    amax = np.abs(w).max(1)
    if fmt == "e4m3":
        byte = np.frexp(amax)[1] - 1 + 127 - 7
    else:
        mant, ex = np.frexp(amax / 6.0)
        byte = np.where(mant > 0.5, ex, ex - 1) + 127
    byte = np.clip(np.where(amax > 0, byte, 1), 1, 254)
    scaled = (w * np.exp2(127.0 - byte)[:, None, :]).reshape(k, n).astype(np.float32)
    by_word = np.ascontiguousarray(scaled.reshape(k // 512, 128, 4, n).transpose(0, 1, 3, 2))
    if fmt == "e4m3":
        words = by_word.astype(ml_dtypes.float8_e4m3fn).view(np.uint8)
    else:
        c = by_word.astype(ml_dtypes.float4_e2m1fn).view(np.uint8) & 0xF
        words = c[..., 0::2] | (c[..., 1::2] << 4)
    return np.ascontiguousarray(words), np.ascontiguousarray(byte.astype(np.uint8).reshape(k // 512, 16, n))


def unpack_weight(words, scales, fmt):
    g, p, n, _ = words.shape
    if fmt == "e4m3":
        vals = np.ascontiguousarray(words).view(ml_dtypes.float8_e4m3fn).astype(np.float64)
    else:
        nib = np.empty((g, p, n, 4), np.uint8)
        nib[..., 0::2] = words & 0xF
        nib[..., 1::2] = words >> 4
        vals = E2M1[nib]
    vals = vals * np.repeat(np.exp2(scales.astype(np.float64) - 127.0), 8, axis=1)[..., None]
    return vals.transpose(0, 1, 3, 2).reshape(g * 512, n)

def pack4(w):
    words, scales = pack_weight(w, "e2m1")
    return words.reshape(words.shape[0], 128, -1), scales


def unpack4(words, scales):
    return unpack_weight(words.reshape(words.shape[0], 128, -1, 2), scales, "e2m1")


B, N, NODE_IN, EDGE_IN, EDGE_OUT = 2, 16, 192, 128, 512
D_IN = 2 * NODE_IN + EDGE_IN
HID = 2 * EDGE_OUT
NEG_SLOPE = 0.1


def leaky_relu(v):
    return np.where(v >= 0.0, v, NEG_SLOPE * v)


def setup_inputs():
    s = mx_kscale(D_IN)
    sn, se = s[:NODE_IN], s[2 * NODE_IN:]
    st = np.concatenate([sn, sn, se])
    node_fts = bf(np.random.standard_normal((B, N, NODE_IN)) * sn)
    edge_fts = bf(np.random.standard_normal((B, N * N, EDGE_IN)) * se)
    wt = np.random.standard_normal((HID, D_IN)) / np.sqrt(D_IN) / st
    words, scales = pack4(np.ascontiguousarray(wt.T))
    return {"node_fts": node_fts,
            "edge_fts": edge_fts,
            "Wt_words": words,
            "Wt_scales": scales}


def reference(node_fts, edge_fts, Wt_words, Wt_scales):
    node = f64(node_fts)
    src = np.repeat(node, N, axis=1)
    dst = np.tile(node, (1, N, 1))
    triplet = np.concatenate([src, dst, f64(edge_fts)], axis=-1)
    return leaky_relu(mxq(triplet, 2, "e4m3") @ unpack4(Wt_words, Wt_scales))

@@ -1,0 +1,121 @@
+import concourse.mybir as mybir
+from concourse.masks import make_identity
+
+F32 = mybir.dt.float32
+BF16 = mybir.dt.bfloat16
+I32 = mybir.dt.int32
+U32 = mybir.dt.uint32
+U8 = mybir.dt.uint8
+FP8X4 = mybir.dt.float8_e4m3fn_x4
+FP4X4 = mybir.dt.float4_e2m1fn_x4
+
+P = 128
+GRAPHS = 2
+NODES = 16
+NODE_IN = 192
+EDGE_IN = 128
+D_IN = 2 * NODE_IN + EDGE_IN
+HID = 1024
+NEG_SLOPE = 0.1
+
+ROWS = GRAPHS * NODES * NODES
+ROW_TILES = ROWS // P
+TILES_PER_GRAPH = ROW_TILES // GRAPHS
+SRC_PER_TILE = P // NODES
+BANK = 512
+HALVES = HID // BANK
+WORDS = D_IN // 2
+LIVE_ROWS = 4
+
+FLOPS = 2 * ROWS * D_IN * HID
+
+
+def tile_edge_update_only_pa_s_kernel(tc, node_fts, edge_fts, Wt_words, Wt_scales, out):
+    nc = tc.nc
+    nodes = node_fts.flatten_outer_dims()
+    out_rows = out.flatten_outer_dims()
+
+    with tc.tile_pool(name="keep", bufs=1) as keep, tc.tile_pool(
+        name="stage", bufs=ROW_TILES
+    ) as stage, tc.tile_pool(name="results", bufs=ROW_TILES * HALVES) as results, tc.psum_pool(
+        name="psum", bufs=8
+    ) as psum:
+        triplets = keep.tile([P, ROW_TILES, D_IN], BF16)
+        w_words = keep.tile([P, 2 * HID], U8, align_bytes=64)
+        w_scales = keep.tile([P, HID], U8, align_bytes=64)
+        t_codes = keep.tile([P, ROW_TILES, P], U32, align_bytes=64)
+        t_scales = keep.tile([P, ROW_TILES, P], U8, align_bytes=64)
+        identity = keep.tile([P, P], F32)
+
+        nc.vector.memset(w_scales[:].bitcast(I32), 0)
+        make_identity(nc, identity[:])
+
+        def load_src(r):
+            rows = nodes[SRC_PER_TILE * r : SRC_PER_TILE * (r + 1), :]
+            nc.sync.dma_start(
+                out=triplets[:, r, 0:NODE_IN],
+                in_=rows.unsqueeze(1).to_broadcast([SRC_PER_TILE, NODES, NODE_IN]),
+            )
+
+        def load_dst(b):
+            nc.sync.dma_start(
+                out=triplets[:, TILES_PER_GRAPH * b, NODE_IN : 2 * NODE_IN],
+                in_=node_fts[b].unsqueeze(0).to_broadcast([SRC_PER_TILE, NODES, NODE_IN]),
+            )
+
+        nc.sync.dma_start(
+            out=triplets[:, :, 2 * NODE_IN : D_IN],
+            in_=edge_fts.rearrange("b (h p) f -> p (b h) f", p=P),
+        )
+        load_src(0)
+        load_dst(0)
+        load_src(1)
+        nc.sync.dma_start(out=w_words[:].bitcast(I32), in_=Wt_words[0].bitcast(I32))
+        for q in range(P // 32):
+            nc.sync.dma_start(
+                out=w_scales[32 * q : 32 * q + LIVE_ROWS, :].bitcast(I32),
+                in_=Wt_scales[0, LIVE_ROWS * q : LIVE_ROWS * (q + 1), :].bitcast(I32),
+            )
+        load_src(2)
+        load_dst(1)
+        load_src(3)
+
+        for r in range(ROW_TILES):
+            if r % TILES_PER_GRAPH == 1:
+                nc.vector.tensor_copy(
+                    out=triplets[:, r, NODE_IN : 2 * NODE_IN],
+                    in_=triplets[:, r - 1, NODE_IN : 2 * NODE_IN],
+                )
+            words = triplets[:, r, :].bitcast(F32)
+            flipped = psum.tile([P, BANK], F32, tag="bank")
+            planes = flipped[:, 0:WORDS].rearrange("p (u m) -> p u m", u=2)
+            for u in range(2):
+                nc.tensor.transpose(planes[:, u, :], words[:, u:WORDS:2], identity[:])
+            grouped = stage.tile([P, 4 * P], BF16, align_bytes=64)
+            nc.scalar.copy(
+                out=grouped[:].bitcast(F32).rearrange("p (m u) -> p m u", u=2),
+                in_=planes.rearrange("p u m -> p m u"),
+            )
+            nc.vector.quantize_mx(
+                out=t_codes[:, r, :].bitcast(FP8X4), scales=t_scales[:, r, :], in_=grouped[:]
+            )
+
+        for r in range(ROW_TILES):
+            for h in range(HALVES):
+                acc = psum.tile([P, BANK], F32, tag="bank")
+                nc.tensor.matmul_mx(
+                    out=acc[:],
+                    lhsT=t_codes[:, r, :].bitcast(FP8X4),
+                    lhsT_scale=t_scales[:, r, :],
+                    rhs=w_words[:, 2 * BANK * h : 2 * BANK * (h + 1)].bitcast(FP4X4),
+                    rhs_scale=w_scales[:, BANK * h : BANK * (h + 1)],
+                    start=True,
+                    stop=True,
+                )
+                tenth = stage.tile([P, BANK], F32)
+                nc.scalar.mul(out=tenth[:], in_=acc[:], mul=NEG_SLOPE)
+                result = results.tile([P, BANK], F32)
+                nc.vector.tensor_max(result[:], acc[:], tenth[:])
+                nc.sync.dma_start(
+                    out=out_rows[P * r : P * (r + 1), BANK * h : BANK * (h + 1)], in_=result[:]
+                )

@@ -26,6 +26,7 @@ BANK = 512
 HALVES = HID // BANK
 WORDS = D_IN // 2
 LIVE_ROWS = 4
+AHEAD = 2
 
 FLOPS = 2 * ROWS * D_IN * HID
 
@@ -63,24 +64,21 @@ def tile_edge_update_only_pa_s_kernel(tc, node_fts, edge_fts, Wt_words, Wt_scale
                 in_=node_fts[b].unsqueeze(0).to_broadcast([SRC_PER_TILE, NODES, NODE_IN]),
             )
 
-        nc.sync.dma_start(
-            out=triplets[:, :, 2 * NODE_IN : D_IN],
-            in_=edge_fts.rearrange("b (h p) f -> p (b h) f", p=P),
-        )
-        load_src(0)
-        load_dst(0)
-        load_src(1)
-        nc.sync.dma_start(out=w_words[:].bitcast(I32), in_=Wt_words[0].bitcast(I32))
-        for q in range(P // 32):
+        def load_edges():
             nc.sync.dma_start(
-                out=w_scales[32 * q : 32 * q + LIVE_ROWS, :].bitcast(I32),
-                in_=Wt_scales[0, LIVE_ROWS * q : LIVE_ROWS * (q + 1), :].bitcast(I32),
+                out=triplets[:, :, 2 * NODE_IN : D_IN],
+                in_=edge_fts.rearrange("b (h p) f -> p (b h) f", p=P),
             )
-        load_src(2)
-        load_dst(1)
-        load_src(3)
 
-        for r in range(ROW_TILES):
+        def load_weight():
+            nc.sync.dma_start(out=w_words[:].bitcast(I32), in_=Wt_words[0].bitcast(I32))
+            for q in range(P // 32):
+                nc.sync.dma_start(
+                    out=w_scales[32 * q : 32 * q + LIVE_ROWS, :].bitcast(I32),
+                    in_=Wt_scales[0, LIVE_ROWS * q : LIVE_ROWS * (q + 1), :].bitcast(I32),
+                )
+
+        def quantise_tile(r):
             if r % TILES_PER_GRAPH == 1:
                 nc.vector.tensor_copy(
                     out=triplets[:, r, NODE_IN : 2 * NODE_IN],
@@ -100,7 +98,7 @@ def tile_edge_update_only_pa_s_kernel(tc, node_fts, edge_fts, Wt_words, Wt_scale
                 out=t_codes[:, r, :].bitcast(FP8X4), scales=t_scales[:, r, :], in_=grouped[:]
             )
 
-        for r in range(ROW_TILES):
+        def multiply_tile(r):
             for h in range(HALVES):
                 acc = psum.tile([P, BANK], F32, tag="bank")
                 nc.tensor.matmul_mx(
@@ -119,3 +117,19 @@ def tile_edge_update_only_pa_s_kernel(tc, node_fts, edge_fts, Wt_words, Wt_scale
                 nc.sync.dma_start(
                     out=out_rows[P * r : P * (r + 1), BANK * h : BANK * (h + 1)], in_=result[:]
                 )
+
+        with tc.manual_schedule():
+            load_src(0)
+            load_dst(0)
+            load_edges()
+            load_src(1)
+            load_weight()
+            load_src(2)
+            load_dst(1)
+            load_src(3)
+            for r in range(AHEAD):
+                quantise_tile(r)
+            for r in range(ROW_TILES):
+                multiply_tile(r)
+                if r + AHEAD < ROW_TILES:
+                    quantise_tile(r + AHEAD)

@@ -19,14 +19,17 @@ HID = 1024
 NEG_SLOPE = 0.1
 
 ROWS = GRAPHS * NODES * NODES
-ROW_TILES = ROWS // P
-TILES_PER_GRAPH = ROW_TILES // GRAPHS
-SRC_PER_TILE = P // NODES
+TILES = ROWS // P
+HALF_P = P // GRAPHS
 BANK = 512
-HALVES = HID // BANK
+FIRST_TILE = (128, 128, 256, BANK)
+MIDDLE_TILE = (BANK, BANK)
+LAST_TILE = (BANK, 256, 128, 128)
 WORDS = D_IN // 2
 LIVE_ROWS = 4
-AHEAD = 2
+SRC = slice(0, NODE_IN)
+DST = slice(NODE_IN, 2 * NODE_IN)
+EDGE = slice(2 * NODE_IN, D_IN)
 
 FLOPS = 2 * ROWS * D_IN * HID
 
@@ -34,41 +37,36 @@ FLOPS = 2 * ROWS * D_IN * HID
 def tile_edge_update_only_pa_s_kernel(tc, node_fts, edge_fts, Wt_words, Wt_scales, out):
     nc = tc.nc
     nodes = node_fts.flatten_outer_dims()
-    out_rows = out.flatten_outer_dims()
+    edge_rows = edge_fts.flatten_outer_dims().rearrange("(p t) f -> p t f", t=TILES)
+    out_rows = out.flatten_outer_dims().rearrange("(p t) n -> p t n", t=TILES)
 
     with tc.tile_pool(name="keep", bufs=1) as keep, tc.tile_pool(
-        name="stage", bufs=ROW_TILES
-    ) as stage, tc.tile_pool(name="results", bufs=ROW_TILES * HALVES) as results, tc.psum_pool(
+        name="stage", bufs=TILES
+    ) as stage, tc.tile_pool(name="results", bufs=len(FIRST_TILE) + len(LAST_TILE) + (TILES - 2) * len(MIDDLE_TILE)) as results, tc.psum_pool(
         name="psum", bufs=8
     ) as psum:
-        triplets = keep.tile([P, ROW_TILES, D_IN], BF16)
+        triplets = keep.tile([P, TILES, D_IN], BF16)
+        dst_nodes = keep.tile([P, TILES, NODE_IN], BF16)
         w_words = keep.tile([P, 2 * HID], U8, align_bytes=64)
         w_scales = keep.tile([P, HID], U8, align_bytes=64)
-        t_codes = keep.tile([P, ROW_TILES, P], U32, align_bytes=64)
-        t_scales = keep.tile([P, ROW_TILES, P], U8, align_bytes=64)
+        t_codes = keep.tile([P, TILES, P], U32, align_bytes=64)
+        t_scales = keep.tile([P, TILES, P], U8, align_bytes=64)
         identity = keep.tile([P, P], F32)
 
-        nc.vector.memset(w_scales[:].bitcast(I32), 0)
-        make_identity(nc, identity[:])
-
-        def load_src(r):
-            rows = nodes[SRC_PER_TILE * r : SRC_PER_TILE * (r + 1), :]
+        def load_triplets():
             nc.sync.dma_start(
-                out=triplets[:, r, 0:NODE_IN],
-                in_=rows.unsqueeze(1).to_broadcast([SRC_PER_TILE, NODES, NODE_IN]),
+                out=triplets[:, 0, SRC],
+                in_=nodes.unsqueeze(1).to_broadcast([GRAPHS * NODES, NODES // TILES, NODE_IN]),
             )
-
-        def load_dst(b):
-            nc.sync.dma_start(
-                out=triplets[:, TILES_PER_GRAPH * b, NODE_IN : 2 * NODE_IN],
-                in_=node_fts[b].unsqueeze(0).to_broadcast([SRC_PER_TILE, NODES, NODE_IN]),
-            )
-
-        def load_edges():
-            nc.sync.dma_start(
-                out=triplets[:, :, 2 * NODE_IN : D_IN],
-                in_=edge_fts.rearrange("b (h p) f -> p (b h) f", p=P),
-            )
+            for b in range(GRAPHS):
+                nc.sync.dma_start(
+                    out=dst_nodes[HALF_P * b : HALF_P * (b + 1), :, :].rearrange("p t f -> p (t f)"),
+                    in_=node_fts[b]
+                    .rearrange("(q t) f -> q (t f)", t=TILES)
+                    .unsqueeze(0)
+                    .to_broadcast([NODES, NODES // TILES, TILES * NODE_IN]),
+                )
+            nc.sync.dma_start(out=triplets[:, :, EDGE], in_=edge_rows)
 
         def load_weight():
             nc.sync.dma_start(out=w_words[:].bitcast(I32), in_=Wt_words[0].bitcast(I32))
@@ -78,13 +76,16 @@ def tile_edge_update_only_pa_s_kernel(tc, node_fts, edge_fts, Wt_words, Wt_scale
                     in_=Wt_scales[0, LIVE_ROWS * q : LIVE_ROWS * (q + 1), :].bitcast(I32),
                 )
 
-        def quantise_tile(r):
-            if r % TILES_PER_GRAPH == 1:
-                nc.vector.tensor_copy(
-                    out=triplets[:, r, NODE_IN : 2 * NODE_IN],
-                    in_=triplets[:, r - 1, NODE_IN : 2 * NODE_IN],
-                )
-            words = triplets[:, r, :].bitcast(F32)
+        def assemble_triplets():
+            nc.vector.tensor_copy(out=triplets[:, 0, DST], in_=dst_nodes[:, 0, :])
+            nc.vector.tensor_copy(out=triplets[:, 1:TILES, DST], in_=dst_nodes[:, 1:TILES, :])
+            nc.vector.tensor_copy(
+                out=triplets[:, 1:TILES, SRC],
+                in_=triplets[:, 0:1, SRC].to_broadcast([P, TILES - 1, NODE_IN]),
+            )
+
+        def quantise_tile(t):
+            words = triplets[:, t, :].bitcast(F32)
             flipped = psum.tile([P, BANK], F32, tag="bank")
             planes = flipped[:, 0:WORDS].rearrange("p (u m) -> p u m", u=2)
             for u in range(2):
@@ -95,41 +96,41 @@ def tile_edge_update_only_pa_s_kernel(tc, node_fts, edge_fts, Wt_words, Wt_scale
                 in_=planes.rearrange("p u m -> p m u"),
             )
             nc.vector.quantize_mx(
-                out=t_codes[:, r, :].bitcast(FP8X4), scales=t_scales[:, r, :], in_=grouped[:]
+                out=t_codes[:, t, :].bitcast(FP8X4), scales=t_scales[:, t, :], in_=grouped[:]
             )
 
-        def multiply_tile(r):
-            for h in range(HALVES):
+        def multiply_tile(t, widths):
+            first = 0
+            for width in widths:
+                last = first + width
                 acc = psum.tile([P, BANK], F32, tag="bank")
                 nc.tensor.matmul_mx(
-                    out=acc[:],
-                    lhsT=t_codes[:, r, :].bitcast(FP8X4),
-                    lhsT_scale=t_scales[:, r, :],
-                    rhs=w_words[:, 2 * BANK * h : 2 * BANK * (h + 1)].bitcast(FP4X4),
-                    rhs_scale=w_scales[:, BANK * h : BANK * (h + 1)],
+                    out=acc[:, 0:width],
+                    lhsT=t_codes[:, t, :].bitcast(FP8X4),
+                    lhsT_scale=t_scales[:, t, :],
+                    rhs=w_words[:, 2 * first : 2 * last].bitcast(FP4X4),
+                    rhs_scale=w_scales[:, first:last],
                     start=True,
                     stop=True,
                 )
                 tenth = stage.tile([P, BANK], F32)
-                nc.scalar.mul(out=tenth[:], in_=acc[:], mul=NEG_SLOPE)
+                nc.scalar.mul(out=tenth[:, 0:width], in_=acc[:, 0:width], mul=NEG_SLOPE)
                 result = results.tile([P, BANK], F32)
-                nc.vector.tensor_max(result[:], acc[:], tenth[:])
-                nc.sync.dma_start(
-                    out=out_rows[P * r : P * (r + 1), BANK * h : BANK * (h + 1)], in_=result[:]
-                )
+                nc.vector.tensor_max(result[:, 0:width], acc[:, 0:width], tenth[:, 0:width])
+                nc.sync.dma_start(out=out_rows[:, t, first:last], in_=result[:, 0:width])
+                first = last
 
-        with tc.manual_schedule():
-            load_src(0)
-            load_dst(0)
-            load_edges()
-            load_src(1)
+        def run():
+            nc.vector.memset(w_scales[:].bitcast(I32), 0)
+            make_identity(nc, identity[:])
+            load_triplets()
             load_weight()
-            load_src(2)
-            load_dst(1)
-            load_src(3)
-            for r in range(AHEAD):
-                quantise_tile(r)
-            for r in range(ROW_TILES):
-                multiply_tile(r)
-                if r + AHEAD < ROW_TILES:
-                    quantise_tile(r + AHEAD)
+            assemble_triplets()
+            for t in range(TILES):
+                quantise_tile(t)
+            multiply_tile(0, FIRST_TILE)
+            for t in range(1, TILES - 1):
+                multiply_tile(t, MIDDLE_TILE)
+            multiply_tile(TILES - 1, LAST_TILE)
+
+        run()

@@ -26,6 +26,7 @@ FIRST_TILE = (128, 128, 256, BANK)
 MIDDLE_TILE = (BANK, BANK)
 LAST_TILE = (BANK, 256, 128, 128)
 WORDS = D_IN // 2
+WARM_UP_PASSES = 3
 LIVE_ROWS = 4
 SRC = slice(0, NODE_IN)
 DST = slice(NODE_IN, 2 * NODE_IN)
@@ -52,6 +53,7 @@ def tile_edge_update_only_pa_s_kernel(tc, node_fts, edge_fts, Wt_words, Wt_scale
         t_codes = keep.tile([P, TILES, P], U32, align_bytes=64)
         t_scales = keep.tile([P, TILES, P], U8, align_bytes=64)
         identity = keep.tile([P, P], F32)
+        idle_work = keep.tile([P, BANK], BF16)
 
         def load_triplets():
             nc.sync.dma_start(
@@ -120,9 +122,16 @@ def tile_edge_update_only_pa_s_kernel(tc, node_fts, edge_fts, Wt_words, Wt_scale
                 nc.sync.dma_start(out=out_rows[:, t, first:last], in_=result[:, 0:width])
                 first = last
 
+        def warm_up():
+            nc.vector.memset(idle_work[:], 0.0)
+            unused = psum.tile([P, BANK], F32, tag="bank")
+            for _ in range(WARM_UP_PASSES):
+                nc.tensor.matmul(out=unused[:], lhsT=idle_work[:, 0:P], rhs=idle_work[:], start=True, stop=True)
+
         def run():
             nc.vector.memset(w_scales[:].bitcast(I32), 0)
             make_identity(nc, identity[:])
+            warm_up()
             load_triplets()
             load_weight()
             assemble_triplets()

@@ -26,7 +26,7 @@ FIRST_TILE = (128, 128, 256, BANK)
 MIDDLE_TILE = (BANK, BANK)
 LAST_TILE = (BANK, 256, 128, 128)
 WORDS = D_IN // 2
-WARM_UP_PASSES = 3
+WARM_UP_PASSES = 6
 LIVE_ROWS = 4
 SRC = slice(0, NODE_IN)
 DST = slice(NODE_IN, 2 * NODE_IN)
@@ -53,7 +53,7 @@ def tile_edge_update_only_pa_s_kernel(tc, node_fts, edge_fts, Wt_words, Wt_scale
         t_codes = keep.tile([P, TILES, P], U32, align_bytes=64)
         t_scales = keep.tile([P, TILES, P], U8, align_bytes=64)
         identity = keep.tile([P, P], F32)
-        idle_work = keep.tile([P, BANK], BF16)
+        idle_work = keep.tile([P, P], F32)
 
         def load_triplets():
             nc.sync.dma_start(
@@ -123,15 +123,15 @@ def tile_edge_update_only_pa_s_kernel(tc, node_fts, edge_fts, Wt_words, Wt_scale
                 first = last
 
         def warm_up():
-            nc.vector.memset(idle_work[:], 0.0)
+            nc.gpsimd.memset(idle_work[:], 0.0)
             unused = psum.tile([P, BANK], F32, tag="bank")
             for _ in range(WARM_UP_PASSES):
-                nc.tensor.matmul(out=unused[:], lhsT=idle_work[:, 0:P], rhs=idle_work[:], start=True, stop=True)
+                nc.tensor.matmul(out=unused[:, 0:P], lhsT=idle_work[:], rhs=idle_work[:], start=True, stop=True)
 
         def run():
             nc.vector.memset(w_scales[:].bitcast(I32), 0)
-            make_identity(nc, identity[:])
             warm_up()
+            make_identity(nc, identity[:])
             load_triplets()
             load_weight()
             assemble_triplets()

@@ -26,7 +26,7 @@ FIRST_TILE = (128, 128, 256, BANK)
 MIDDLE_TILE = (BANK, BANK)
 LAST_TILE = (BANK, 256, 128, 128)
 WORDS = D_IN // 2
-WARM_UP_PASSES = 6
+WARM_UP_PASSES = 5
 LIVE_ROWS = 4
 SRC = slice(0, NODE_IN)
 DST = slice(NODE_IN, 2 * NODE_IN)

@@ -38,7 +38,7 @@ FLOPS = 2 * ROWS * D_IN * HID
 def tile_edge_update_only_pa_s_kernel(tc, node_fts, edge_fts, Wt_words, Wt_scales, out):
     nc = tc.nc
     nodes = node_fts.flatten_outer_dims()
-    edge_rows = edge_fts.flatten_outer_dims().rearrange("(p t) f -> p t f", t=TILES)
+    edge_rows = edge_fts.flatten_outer_dims().rearrange("(p t) f -> p (t f)", t=TILES)
     out_rows = out.flatten_outer_dims().rearrange("(p t) n -> p t n", t=TILES)
 
     with tc.tile_pool(name="keep", bufs=1) as keep, tc.tile_pool(
@@ -46,7 +46,8 @@ def tile_edge_update_only_pa_s_kernel(tc, node_fts, edge_fts, Wt_words, Wt_scale
     ) as stage, tc.tile_pool(name="results", bufs=len(FIRST_TILE) + len(LAST_TILE) + (TILES - 2) * len(MIDDLE_TILE)) as results, tc.psum_pool(
         name="psum", bufs=8
     ) as psum:
-        triplets = keep.tile([P, TILES, D_IN], BF16)
+        first = keep.tile([P, D_IN + (TILES - 1) * EDGE_IN], BF16)
+        later = keep.tile([P, TILES - 1, D_IN], BF16)
         dst_nodes = keep.tile([P, TILES, NODE_IN], BF16)
         w_words = keep.tile([P, 2 * HID], U8, align_bytes=64)
         w_scales = keep.tile([P, HID], U8, align_bytes=64)
@@ -57,7 +58,7 @@ def tile_edge_update_only_pa_s_kernel(tc, node_fts, edge_fts, Wt_words, Wt_scale
 
         def load_triplets():
             nc.sync.dma_start(
-                out=triplets[:, 0, SRC],
+                out=first[:, SRC],
                 in_=nodes.unsqueeze(1).to_broadcast([GRAPHS * NODES, NODES // TILES, NODE_IN]),
             )
             for b in range(GRAPHS):
@@ -68,7 +69,7 @@ def tile_edge_update_only_pa_s_kernel(tc, node_fts, edge_fts, Wt_words, Wt_scale
                     .unsqueeze(0)
                     .to_broadcast([NODES, NODES // TILES, TILES * NODE_IN]),
                 )
-            nc.sync.dma_start(out=triplets[:, :, EDGE], in_=edge_rows)
+            nc.sync.dma_start(out=first[:, 2 * NODE_IN :], in_=edge_rows)
 
         def load_weight():
             nc.sync.dma_start(out=w_words[:].bitcast(I32), in_=Wt_words[0].bitcast(I32))
@@ -79,15 +80,16 @@ def tile_edge_update_only_pa_s_kernel(tc, node_fts, edge_fts, Wt_words, Wt_scale
                 )
 
         def assemble_triplets():
-            nc.vector.tensor_copy(out=triplets[:, 0, DST], in_=dst_nodes[:, 0, :])
-            nc.vector.tensor_copy(out=triplets[:, 1:TILES, DST], in_=dst_nodes[:, 1:TILES, :])
+            nc.vector.tensor_copy(out=first[:, DST], in_=dst_nodes[:, 0, :])
+            nc.scalar.copy(out=later[:, :, EDGE], in_=first[:, D_IN:].rearrange("p (t f) -> p t f", f=EDGE_IN))
+            nc.vector.tensor_copy(out=later[:, :, DST], in_=dst_nodes[:, 1:TILES, :])
             nc.vector.tensor_copy(
-                out=triplets[:, 1:TILES, SRC],
-                in_=triplets[:, 0:1, SRC].to_broadcast([P, TILES - 1, NODE_IN]),
+                out=later[:, :, SRC],
+                in_=first[:, SRC].unsqueeze(1).to_broadcast([P, TILES - 1, NODE_IN]),
             )
 
         def quantise_tile(t):
-            words = triplets[:, t, :].bitcast(F32)
+            words = (first[:, 0:D_IN] if t == 0 else later[:, t - 1, :]).bitcast(F32)
             flipped = psum.tile([P, BANK], F32, tag="bank")
             planes = flipped[:, 0:WORDS].rearrange("p (u m) -> p u m", u=2)
             for u in range(2):

@@ -124,6 +124,10 @@ def tile_edge_update_only_pa_s_kernel(tc, node_fts, edge_fts, Wt_words, Wt_scale
                 nc.sync.dma_start(out=out_rows[:, t, first:last], in_=result[:, 0:width])
                 first = last
 
+        def keep_warm():
+            unused = psum.tile([P, BANK], F32, tag="bank")
+            nc.tensor.matmul(out=unused[:, 0:P], lhsT=idle_work[:], rhs=idle_work[:], start=True, stop=True)
+
         def warm_up():
             nc.gpsimd.memset(idle_work[:], 0.0)
             unused = psum.tile([P, BANK], F32, tag="bank")
@@ -139,9 +143,11 @@ def tile_edge_update_only_pa_s_kernel(tc, node_fts, edge_fts, Wt_words, Wt_scale
             assemble_triplets()
             for t in range(TILES):
                 quantise_tile(t)
+            keep_warm()
             multiply_tile(0, FIRST_TILE)
             for t in range(1, TILES - 1):
                 multiply_tile(t, MIDDLE_TILE)
             multiply_tile(TILES - 1, LAST_TILE)
 
-        run()
+        with tc.manual_schedule(engines={mybir.EngineType.PE}):
+            run()

@@ -24,7 +24,7 @@ HALF_P = P // GRAPHS
 BANK = 512
 FIRST_TILE = (128, 128, 256, BANK)
 MIDDLE_TILE = (BANK, BANK)
-LAST_TILE = (BANK, 256, 128, 128)
+LAST_TILE = (BANK, BANK)
 WORDS = D_IN // 2
 WARM_UP_PASSES = 5
 LIVE_ROWS = 4

import concourse.mybir as mybir
from concourse.masks import make_identity

F32 = mybir.dt.float32
BF16 = mybir.dt.bfloat16
I32 = mybir.dt.int32
U32 = mybir.dt.uint32
U8 = mybir.dt.uint8
FP8X4 = mybir.dt.float8_e4m3fn_x4
FP4X4 = mybir.dt.float4_e2m1fn_x4

P = 128
GRAPHS = 2
NODES = 16
NODE_IN = 192
EDGE_IN = 128
D_IN = 2 * NODE_IN + EDGE_IN
HID = 1024
NEG_SLOPE = 0.1

ROWS = GRAPHS * NODES * NODES
TILES = ROWS // P
HALF_P = P // GRAPHS
BANK = 512
FIRST_TILE = (128, 128, 256, BANK)
MIDDLE_TILE = (BANK, BANK)
LAST_TILE = (BANK, BANK)
WORDS = D_IN // 2
WARM_UP_PASSES = 5
LIVE_ROWS = 4
SRC = slice(0, NODE_IN)
DST = slice(NODE_IN, 2 * NODE_IN)
EDGE = slice(2 * NODE_IN, D_IN)

FLOPS = 2 * ROWS * D_IN * HID


def tile_edge_update_only_pa_s_kernel(tc, node_fts, edge_fts, Wt_words, Wt_scales, out):
    nc = tc.nc
    nodes = node_fts.flatten_outer_dims()
    edge_rows = edge_fts.flatten_outer_dims().rearrange("(p t) f -> p (t f)", t=TILES)
    out_rows = out.flatten_outer_dims().rearrange("(p t) n -> p t n", t=TILES)

    with tc.tile_pool(name="keep", bufs=1) as keep, tc.tile_pool(
        name="stage", bufs=TILES
    ) as stage, tc.tile_pool(name="results", bufs=len(FIRST_TILE) + len(LAST_TILE) + (TILES - 2) * len(MIDDLE_TILE)) as results, tc.psum_pool(
        name="psum", bufs=8
    ) as psum:
        first = keep.tile([P, D_IN + (TILES - 1) * EDGE_IN], BF16)
        later = keep.tile([P, TILES - 1, D_IN], BF16)
        dst_nodes = keep.tile([P, TILES, NODE_IN], BF16)
        w_words = keep.tile([P, 2 * HID], U8, align_bytes=64)
        w_scales = keep.tile([P, HID], U8, align_bytes=64)
        t_codes = keep.tile([P, TILES, P], U32, align_bytes=64)
        t_scales = keep.tile([P, TILES, P], U8, align_bytes=64)
        identity = keep.tile([P, P], F32)
        idle_work = keep.tile([P, P], F32)

        def load_triplets():
            nc.sync.dma_start(
                out=first[:, SRC],
                in_=nodes.unsqueeze(1).to_broadcast([GRAPHS * NODES, NODES // TILES, NODE_IN]),
            )
            for b in range(GRAPHS):
                nc.sync.dma_start(
                    out=dst_nodes[HALF_P * b : HALF_P * (b + 1), :, :].rearrange("p t f -> p (t f)"),
                    in_=node_fts[b]
                    .rearrange("(q t) f -> q (t f)", t=TILES)
                    .unsqueeze(0)
                    .to_broadcast([NODES, NODES // TILES, TILES * NODE_IN]),
                )
            nc.sync.dma_start(out=first[:, 2 * NODE_IN :], in_=edge_rows)

        def load_weight():
            nc.sync.dma_start(out=w_words[:].bitcast(I32), in_=Wt_words[0].bitcast(I32))
            for q in range(P // 32):
                nc.sync.dma_start(
                    out=w_scales[32 * q : 32 * q + LIVE_ROWS, :].bitcast(I32),
                    in_=Wt_scales[0, LIVE_ROWS * q : LIVE_ROWS * (q + 1), :].bitcast(I32),
                )

        def assemble_triplets():
            nc.vector.tensor_copy(out=first[:, DST], in_=dst_nodes[:, 0, :])
            nc.scalar.copy(out=later[:, :, EDGE], in_=first[:, D_IN:].rearrange("p (t f) -> p t f", f=EDGE_IN))
            nc.vector.tensor_copy(out=later[:, :, DST], in_=dst_nodes[:, 1:TILES, :])
            nc.vector.tensor_copy(
                out=later[:, :, SRC],
                in_=first[:, SRC].unsqueeze(1).to_broadcast([P, TILES - 1, NODE_IN]),
            )

        def quantise_tile(t):
            words = (first[:, 0:D_IN] if t == 0 else later[:, t - 1, :]).bitcast(F32)
            flipped = psum.tile([P, BANK], F32, tag="bank")
            planes = flipped[:, 0:WORDS].rearrange("p (u m) -> p u m", u=2)
            for u in range(2):
                nc.tensor.transpose(planes[:, u, :], words[:, u:WORDS:2], identity[:])
            grouped = stage.tile([P, 4 * P], BF16, align_bytes=64)
            nc.scalar.copy(
                out=grouped[:].bitcast(F32).rearrange("p (m u) -> p m u", u=2),
                in_=planes.rearrange("p u m -> p m u"),
            )
            nc.vector.quantize_mx(
                out=t_codes[:, t, :].bitcast(FP8X4), scales=t_scales[:, t, :], in_=grouped[:]
            )

        def multiply_tile(t, widths):
            first = 0
            for width in widths:
                last = first + width
                acc = psum.tile([P, BANK], F32, tag="bank")
                nc.tensor.matmul_mx(
                    out=acc[:, 0:width],
                    lhsT=t_codes[:, t, :].bitcast(FP8X4),
                    lhsT_scale=t_scales[:, t, :],
                    rhs=w_words[:, 2 * first : 2 * last].bitcast(FP4X4),
                    rhs_scale=w_scales[:, first:last],
                    start=True,
                    stop=True,
                )
                tenth = stage.tile([P, BANK], F32)
                nc.scalar.mul(out=tenth[:, 0:width], in_=acc[:, 0:width], mul=NEG_SLOPE)
                result = results.tile([P, BANK], F32)
                nc.vector.tensor_max(result[:, 0:width], acc[:, 0:width], tenth[:, 0:width])
                nc.sync.dma_start(out=out_rows[:, t, first:last], in_=result[:, 0:width])
                first = last

        def keep_warm():
            unused = psum.tile([P, BANK], F32, tag="bank")
            nc.tensor.matmul(out=unused[:, 0:P], lhsT=idle_work[:], rhs=idle_work[:], start=True, stop=True)

        def warm_up():
            nc.gpsimd.memset(idle_work[:], 0.0)
            unused = psum.tile([P, BANK], F32, tag="bank")
            for _ in range(WARM_UP_PASSES):
                nc.tensor.matmul(out=unused[:, 0:P], lhsT=idle_work[:], rhs=idle_work[:], start=True, stop=True)

        def run():
            nc.vector.memset(w_scales[:].bitcast(I32), 0)
            warm_up()
            make_identity(nc, identity[:])
            load_triplets()
            load_weight()
            assemble_triplets()
            for t in range(TILES):
                quantise_tile(t)
            keep_warm()
            multiply_tile(0, FIRST_TILE)
            for t in range(1, TILES - 1):
                multiply_tile(t, MIDDLE_TILE)
            multiply_tile(TILES - 1, LAST_TILE)

        with tc.manual_schedule(engines={mybir.EngineType.PE}):
            run()
